import numpy as np
import ml_dtypes


def mxq(x, axis, fmt="e4m3"):
    dtype, down = {"e4m3": (ml_dtypes.float8_e4m3fn, 7), "e5m2": (ml_dtypes.float8_e5m2, 14)}[fmt]
    v = np.moveaxis(np.asarray(x, np.float32).astype(ml_dtypes.bfloat16).astype(np.float64), axis, -1)
    blocks = v.reshape(v.shape[:-1] + (-1, 32))
    amax = np.abs(blocks).max(-1, keepdims=True)
    byte = np.maximum(np.where(amax > 0, np.frexp(amax)[1] - 1 + 127, 0) - down, 1)
    scale = np.exp2(byte - 127.0)
    codes = (blocks / scale).astype(np.float32).astype(dtype).astype(np.float64)
    return np.moveaxis((codes * scale).reshape(v.shape), -1, axis)


WIDE = False


def mx_kscale(k):
    if not WIDE:
        return np.ones(k)
    levels = np.array([10, -10, 5, -5, 0])
    if k % 512:
        return np.exp2(np.random.permutation(np.resize(levels, k // 32))).repeat(32)
    a = np.empty((k // 512, 16))
    for p in range(k // 512):
        a[p, :8] = np.random.permutation(np.resize(levels, 8))
        for g in range(8):
            far = levels[np.abs(levels - a[p, g]) >= 10]
            a[p, g + 8] = far[np.random.randint(len(far))]
    return np.exp2(a.ravel()).repeat(32)


BF16 = ml_dtypes.bfloat16


def bf(x):
    return np.asarray(x, np.float32).astype(BF16)


def f64(x):
    return np.asarray(x).astype(np.float64)


B, T, D, H, KV, DH = 4, 2048, 1024, 2, 1, 32
G = H // KV
HALF = DH // 2
ROPE_THETA = 1e6
YARN_FACTOR = 64.0
ORIG_MAX_POS = 4096.0
BETA_FAST, BETA_SLOW = 4.0, 1.0
ATTN_FACTOR = 0.1 * np.log(YARN_FACTOR) + 1.0


def corr_dim(num_rot):
    return DH * np.log(ORIG_MAX_POS / (num_rot * 2 * np.pi)) / (2 * np.log(ROPE_THETA))


def yarn_inv_freq():
    low = float(np.sum(np.arange(DH) + 1 <= corr_dim(BETA_FAST)))
    high = min(float(np.sum(np.arange(DH) < corr_dim(BETA_SLOW))), DH - 1.0)
    if low == high:
        high += 0.001
    ramp = np.clip((np.arange(HALF) - low) / (high - low), 0.0, 1.0)
    pos_freqs = ROPE_THETA ** (np.arange(0, DH, 2) / DH)
    inv_extrap = 1.0 / pos_freqs
    inv_interp = 1.0 / (YARN_FACTOR * pos_freqs)
    extrap_factor = 1.0 - ramp
    return inv_interp * (1.0 - extrap_factor) + inv_extrap * extrap_factor


def rope_yarn(v):
    angles = np.arange(T)[:, None] * yarn_inv_freq()[None, :]
    cos = np.cos(angles)[None, :, None, :]
    sin = np.sin(angles)[None, :, None, :]
    v_even = v[..., 0::2]
    v_odd = v[..., 1::2]
    out_even = v_even * cos - v_odd * sin
    out_odd = v_even * sin + v_odd * cos
    return np.stack([out_even, out_odd], axis=-1).reshape(v.shape) * ATTN_FACTOR


def setup_inputs():
    s = mx_kscale(D)
    return {"x": bf(np.random.standard_normal((B, T, D)) * s),
            "w_qkv": bf(np.random.standard_normal((D, (H + 2 * KV) * DH)) / np.sqrt(D) / s[:, None])}


def reference(x, w_qkv):
    qkv = mxq(f64(x), 2, "e4m3") @ mxq(f64(w_qkv), 0, "e4m3")
    q = qkv[:, :, :H * DH].reshape(B, T, H, DH)
    k = qkv[:, :, H * DH:(H + KV) * DH].reshape(B, T, KV, DH)
    v = qkv[:, :, (H + KV) * DH:].reshape(B, T, KV, DH)
    q = rope_yarn(q)
    k = rope_yarn(k)
    q = q.reshape(B, T, KV, G, DH).transpose(0, 2, 3, 1, 4)
    k = k.transpose(0, 2, 1, 3)
    v = v.transpose(0, 2, 1, 3)
    return q, k, v

@@ -1,0 +1,290 @@
+import math
+from contextlib import ExitStack
+
+import concourse.mybir as mybir
+from concourse.masks import make_identity
+
+F32 = mybir.dt.float32
+BF16 = mybir.dt.bfloat16
+I32 = mybir.dt.int32
+U32 = mybir.dt.uint32
+U8 = mybir.dt.uint8
+FP8X4 = mybir.dt.float8_e4m3fn_x4
+ALU = mybir.AluOpType
+ACT = mybir.ActivationFunctionType
+
+P = 128
+BATCH = 4
+SEQ = 2048
+D_MODEL = 1024
+HEAD_DIM = 32
+PAIRS = HEAD_DIM // 2
+ROPE_HEADS = 3
+HEADS = 4
+FEATURES = HEADS * HEAD_DIM
+ROPE_COLS = ROPE_HEADS * HEAD_DIM
+
+PACK = 4
+K_PASS = P * PACK
+PASSES = D_MODEL // K_PASS
+WORD_BLOCKS = 2
+
+TILES = SEQ // P
+CHUNK_TILES = 4
+CHUNKS = TILES // CHUNK_TILES
+QUANT_TILES = 2
+STORE_CHUNKS = 2
+STORE_TILES = STORE_CHUNKS * CHUNK_TILES
+ALL_CHUNKS = BATCH * CHUNKS
+HALVES = CHUNK_TILES // QUANT_TILES
+STORES = ALL_CHUNKS // STORE_CHUNKS
+
+ROPE_THETA = 1e6
+YARN_FACTOR = 64.0
+RAMP_LOW = 5.0
+RAMP_HIGH = 8.0
+ATTN_FACTOR = 0.1 * math.log(YARN_FACTOR) + 1.0
+TURN_GRID = 2.0**15
+ROUND_MAGIC = 1.5 * 2.0**23
+
+FLOPS = 2 * BATCH * SEQ * D_MODEL * FEATURES
+
+
+def turns_per_position(i):
+    base = ROPE_THETA ** (-i / PAIRS)
+    ramp = min(max((i - RAMP_LOW) / (RAMP_HIGH - RAMP_LOW), 0.0), 1.0)
+    return (base * (1.0 - ramp) + (base / YARN_FACTOR) * ramp) / (2.0 * math.pi)
+
+
+def build_rope_versines(nc, pool):
+    pos_int = pool.tile([P, TILES], I32)
+    nc.gpsimd.iota(pos_int[:], pattern=[[1, TILES]], base=0, channel_multiplier=TILES)
+    pos = pool.tile([P, TILES], F32)
+    nc.vector.tensor_copy(out=pos[:], in_=pos_int[:])
+    sin_first = pool.tile([P, 1], F32)
+    nc.scalar.activation(out=sin_first[:], in_=pos[:, 0:1], func=ACT.Sin, scale=0.0)
+
+    coarse = pool.tile([P, PAIRS, TILES], F32)
+    fine = pool.tile([P, PAIRS, TILES], F32)
+    for i in range(PAIRS):
+        turns = turns_per_position(i)
+        turns_coarse = round(turns * TURN_GRID) / TURN_GRID
+        nc.vector.tensor_scalar(
+            out=coarse[:, i, :], in0=pos[:], scalar1=turns_coarse, scalar2=None, op0=ALU.mult
+        )
+        nc.scalar.mul(out=fine[:, i, :], in_=pos[:], mul=turns - turns_coarse)
+
+    whole = pool.tile([P, PAIRS, TILES], F32)
+    nc.vector.tensor_scalar(
+        out=whole[:],
+        in0=coarse[:],
+        scalar1=ROUND_MAGIC,
+        scalar2=ROUND_MAGIC,
+        op0=ALU.add,
+        op1=ALU.subtract,
+    )
+    frac = pool.tile([P, 3, PAIRS, TILES], F32)
+    nc.vector.tensor_tensor(out=frac[:, 0], in0=coarse[:], in1=whole[:], op=ALU.subtract)
+    nc.vector.tensor_tensor(out=frac[:, 0], in0=frac[:, 0], in1=fine[:], op=ALU.add)
+    nc.vector.tensor_scalar(out=frac[:, 1], in0=frac[:, 0], scalar1=0.25, scalar2=None, op0=ALU.add)
+    nc.vector.tensor_scalar(out=frac[:, 2], in0=frac[:, 0], scalar1=-0.25, scalar2=None, op0=ALU.add)
+
+    versine = pool.tile([P, 3, PAIRS, TILES], F32)
+    nc.scalar.activation(out=versine[:], in_=frac[:], func=ACT.Sin, scale=math.pi)
+    nc.scalar.activation(
+        out=versine[:], in_=versine[:], func=ACT.Square, scale=math.sqrt(2.0 * ATTN_FACTOR)
+    )
+    return versine
+
+
+def finish_rope_tables(nc, versine, cos_tab, sin_tab):
+    nc.vector.tensor_scalar(
+        out=cos_tab[:],
+        in0=versine[:, 0].rearrange("p i j -> p j i").unsqueeze(3).to_broadcast([P, TILES, PAIRS, 2]),
+        scalar1=-1.0,
+        scalar2=ATTN_FACTOR,
+        op0=ALU.mult,
+        op1=ALU.add,
+    )
+    nc.vector.tensor_scalar(
+        out=sin_tab[:],
+        in0=versine[:, 1:3].rearrange("p s i j -> p j i s"),
+        scalar1=-1.0,
+        scalar2=ATTN_FACTOR,
+        op0=ALU.mult,
+        op1=ALU.add,
+    )
+
+
+def tile_causalselfattentiongqa_pa_t_kernel(tc, x, w_qkv, out_0, out_1, out_2):
+    nc = tc.nc
+    with ExitStack() as ctx:
+        const = ctx.enter_context(tc.tile_pool(name="const", bufs=1))
+        x_pool = ctx.enter_context(tc.tile_pool(name="x", bufs=ALL_CHUNKS))
+        mx_pool = ctx.enter_context(tc.tile_pool(name="mx", bufs=3))
+        rope_pool = ctx.enter_context(tc.tile_pool(name="rope", bufs=3))
+        out_pool = ctx.enter_context(tc.tile_pool(name="out", bufs=STORES))
+        psum_t = ctx.enter_context(tc.psum_pool(name="psum_t", bufs=6))
+        psum_u = ctx.enter_context(tc.psum_pool(name="psum_u", bufs=2))
+        ctx.enter_context(tc.manual_schedule())
+
+        x_rows = x.rearrange("b (p j) d -> b p (j d)", j=TILES)
+        x_chunks = {}
+        mx_tiles = {}
+        u_banks = {}
+        rope_tiles = {}
+        out_tiles = {}
+
+        def load(n, parts):
+            b, c = divmod(n, CHUNKS)
+            x_chunk = x_pool.tile([P, CHUNK_TILES * D_MODEL], BF16)
+            width = CHUNK_TILES * D_MODEL // parts
+            for part in range(parts):
+                lo = part * width
+                first = c * CHUNK_TILES * D_MODEL + lo
+                nc.sync.dma_start(out=x_chunk[:, lo : lo + width], in_=x_rows[b, :, first : first + width])
+            x_chunks[n] = x_chunk
+
+        def transpose_and_quantise(n, half):
+            if half == 0:
+                grouped = mx_pool.tile([P, CHUNK_TILES * PASSES * P * PACK], BF16, align_bytes=64)
+                codes = mx_pool.tile([P, CHUNK_TILES * PASSES * P], U32, align_bytes=64)
+                scales = mx_pool.tile([P, CHUNK_TILES * PASSES * P], U8, align_bytes=64)
+                mx_tiles[n] = (grouped, codes, scales)
+            grouped, codes, scales = mx_tiles[n]
+            x_words = x_chunks[n][:].bitcast(F32)
+            grouped_words = grouped[:].bitcast(F32).rearrange(
+                "p (j g c u) -> p j g c u", j=CHUNK_TILES, g=PASSES, u=WORD_BLOCKS
+            )
+            for jj in range(half * QUANT_TILES, (half + 1) * QUANT_TILES):
+                xt = psum_t.tile([P, PASSES, WORD_BLOCKS, P], F32)
+                for g in range(PASSES):
+                    for u in range(WORD_BLOCKS):
+                        first = (jj * PASSES + g) * WORD_BLOCKS * P
+                        words = x_words[:, first + u : first + WORD_BLOCKS * P : WORD_BLOCKS]
+                        nc.tensor.transpose(xt[:, g, u, :], words, identity[:])
+                nc.scalar.copy(out=grouped_words[:, jj], in_=xt[:].rearrange("p g u c -> p g c u"))
+            words = QUANT_TILES * PASSES * P
+            lo = half * words
+            nc.vector.quantize_mx(
+                out=codes[:, lo : lo + words].bitcast(FP8X4),
+                scales=scales[:, lo : lo + words],
+                in_=grouped[:, lo * PACK : (lo + words) * PACK],
+            )
+
+        def project(n):
+            grouped, codes, scales = mx_tiles[n]
+            u_bank = psum_u.tile([P, CHUNK_TILES, FEATURES], F32)
+            for jj in range(CHUNK_TILES):
+                for g in range(PASSES):
+                    lo = (jj * PASSES + g) * P
+                    nc.tensor.matmul_mx(
+                        out=u_bank[:, jj, :],
+                        lhsT=codes[:, lo : lo + P].bitcast(FP8X4),
+                        lhsT_scale=scales[:, lo : lo + P],
+                        rhs=w_codes[:, g * FEATURES : (g + 1) * FEATURES].bitcast(FP8X4),
+                        rhs_scale=w_scales[:, g * FEATURES : (g + 1) * FEATURES],
+                        start=(g == 0),
+                        stop=(g == PASSES - 1),
+                    )
+            u_banks[n] = u_bank
+
+        def rope_products(n):
+            c = n % CHUNKS
+            if c % STORE_CHUNKS == 0:
+                out_sb = out_pool.tile([P, HEADS, STORE_TILES, HEAD_DIM], F32)
+                out_tiles[n // STORE_CHUNKS] = out_sb
+            out_sb = out_tiles[n // STORE_CHUNKS]
+            u_bank = u_banks[n]
+            j_batch = c * CHUNK_TILES
+            j_store = (c % STORE_CHUNKS) * CHUNK_TILES
+            nc.scalar.copy(
+                out=out_sb[:, ROPE_HEADS, j_store : j_store + CHUNK_TILES, :],
+                in_=u_bank[:, :, ROPE_COLS:],
+            )
+            roped = u_bank[:, :, :ROPE_COLS]
+            by_cos = rope_pool.tile([P, CHUNK_TILES, ROPE_HEADS, HEAD_DIM], F32)
+            nc.vector.tensor_tensor(
+                out=by_cos[:],
+                in0=roped.rearrange("p j (h d) -> p j h d", h=ROPE_HEADS),
+                in1=cos_tab[:, j_batch : j_batch + CHUNK_TILES]
+                .rearrange("p j i two -> p j (i two)")
+                .unsqueeze(2)
+                .to_broadcast([P, CHUNK_TILES, ROPE_HEADS, HEAD_DIM]),
+                op=ALU.mult,
+            )
+            by_sin = rope_pool.tile([P, CHUNK_TILES, ROPE_HEADS, PAIRS, 2], F32)
+            nc.vector.tensor_tensor(
+                out=by_sin[:],
+                in0=roped.rearrange("p j (h i two) -> p j h i two", h=ROPE_HEADS, two=2)[:, :, :, :, ::-1],
+                in1=sin_tab[:, j_batch : j_batch + CHUNK_TILES]
+                .unsqueeze(2)
+                .to_broadcast([P, CHUNK_TILES, ROPE_HEADS, PAIRS, 2]),
+                op=ALU.mult,
+            )
+            rope_tiles[n] = (by_cos, by_sin)
+
+        def rope_sum_and_store(n):
+            b, c = divmod(n, CHUNKS)
+            out_sb = out_tiles[n // STORE_CHUNKS]
+            by_cos, by_sin = rope_tiles[n]
+            j_store = (c % STORE_CHUNKS) * CHUNK_TILES
+            nc.vector.tensor_tensor(
+                out=out_sb[:, :ROPE_HEADS, j_store : j_store + CHUNK_TILES, :].rearrange("p h j d -> p j h d"),
+                in0=by_cos[:],
+                in1=by_sin[:].rearrange("p j h i two -> p j h (i two)"),
+                op=ALU.add,
+            )
+            if c % STORE_CHUNKS == STORE_CHUNKS - 1:
+                j0 = (c + 1) * CHUNK_TILES - STORE_TILES
+                nc.sync.dma_start(
+                    out=out_0[b, 0].rearrange("h (p j) d -> p h j d", j=TILES)[:, :, j0 : j0 + STORE_TILES, :],
+                    in_=out_sb[:, 0:2],
+                )
+                nc.sync.dma_start(
+                    out=out_1[b, 0].rearrange("(p j) d -> p j d", j=TILES)[:, j0 : j0 + STORE_TILES, :],
+                    in_=out_sb[:, 2],
+                )
+                nc.sync.dma_start(
+                    out=out_2[b, 0].rearrange("(p j) d -> p j d", j=TILES)[:, j0 : j0 + STORE_TILES, :],
+                    in_=out_sb[:, 3],
+                )
+
+        load(0, HALVES)
+        w_raw = const.tile([P, PASSES, PACK, FEATURES], BF16)
+        nc.sync.dma_start(
+            out=w_raw[:].rearrange("p g t c -> p g (t c)"),
+            in_=w_qkv.rearrange("(g p t) c -> p g (t c)", p=P, t=PACK),
+        )
+        for n in range(1, ALL_CHUNKS):
+            load(n, 1)
+
+        versine = build_rope_versines(nc, const)
+
+        identity = const.tile([P, P], F32)
+        make_identity(nc, identity[:])
+
+        w_grouped = const.tile([P, PASSES, FEATURES, PACK], BF16, align_bytes=64)
+        nc.vector.tensor_copy(out=w_grouped[:], in_=w_raw[:].rearrange("p g t c -> p g c t"))
+        w_codes = const.tile([P, PASSES * FEATURES], U32, align_bytes=64)
+        w_scales = const.tile([P, PASSES * FEATURES], U8, align_bytes=64)
+        nc.vector.quantize_mx(
+            out=w_codes[:].bitcast(FP8X4),
+            scales=w_scales[:],
+            in_=w_grouped[:].rearrange("p g c t -> p (g c t)"),
+        )
+
+        cos_tab = const.tile([P, TILES, PAIRS, 2], F32)
+        sin_tab = const.tile([P, TILES, PAIRS, 2], F32)
+        finish_rope_tables(nc, versine, cos_tab, sin_tab)
+
+        for n in range(ALL_CHUNKS + 2):
+            if n < ALL_CHUNKS:
+                transpose_and_quantise(n, 0)
+            if 0 <= n - 2:
+                rope_sum_and_store(n - 2)
+            if n < ALL_CHUNKS:
+                transpose_and_quantise(n, 1)
+            if 0 <= n - 1 < ALL_CHUNKS:
+                project(n - 1)
+                rope_products(n - 1)

@@ -32,11 +32,14 @@ WORD_BLOCKS = 2
 TILES = SEQ // P
 CHUNK_TILES = 4
 CHUNKS = TILES // CHUNK_TILES
-QUANT_TILES = 2
+HALF_TILES = CHUNK_TILES // 2
+PASS_WORDS = WORD_BLOCKS * P
+TILE_WORDS = PASSES * PASS_WORDS
 STORE_CHUNKS = 2
 STORE_TILES = STORE_CHUNKS * CHUNK_TILES
 ALL_CHUNKS = BATCH * CHUNKS
-HALVES = CHUNK_TILES // QUANT_TILES
+HALVES = 2
+EARLY_CHUNKS = 5
 STORES = ALL_CHUNKS // STORE_CHUNKS
 
 ROPE_THETA = 1e6
@@ -56,25 +59,36 @@ def turns_per_position(i):
     return (base * (1.0 - ramp) + (base / YARN_FACTOR) * ramp) / (2.0 * math.pi)
 
 
-def build_rope_versines(nc, pool):
+def build_positions(nc, pool):
     pos_int = pool.tile([P, TILES], I32)
     nc.gpsimd.iota(pos_int[:], pattern=[[1, TILES]], base=0, channel_multiplier=TILES)
     pos = pool.tile([P, TILES], F32)
     nc.vector.tensor_copy(out=pos[:], in_=pos_int[:])
+    return pos
+
+
+def build_rope_versines(nc, pool, pos):
     sin_first = pool.tile([P, 1], F32)
     nc.scalar.activation(out=sin_first[:], in_=pos[:, 0:1], func=ACT.Sin, scale=0.0)
 
-    coarse = pool.tile([P, PAIRS, TILES], F32)
-    fine = pool.tile([P, PAIRS, TILES], F32)
+    turns = [turns_per_position(i) for i in range(PAIRS)]
+    coarse_turns = [round(t * TURN_GRID) / TURN_GRID for t in turns]
+    fast = sum(t != 0.0 for t in coarse_turns)
+    coarse = pool.tile([P, fast, TILES], F32)
+    fine = pool.tile([P, fast, TILES], F32)
+    frac = pool.tile([P, 3, PAIRS, TILES], F32)
     for i in range(PAIRS):
-        turns = turns_per_position(i)
-        turns_coarse = round(turns * TURN_GRID) / TURN_GRID
-        nc.vector.tensor_scalar(
-            out=coarse[:, i, :], in0=pos[:], scalar1=turns_coarse, scalar2=None, op0=ALU.mult
-        )
-        nc.scalar.mul(out=fine[:, i, :], in_=pos[:], mul=turns - turns_coarse)
+        if i < fast:
+            nc.vector.tensor_scalar(
+                out=coarse[:, i, :], in0=pos[:], scalar1=coarse_turns[i], scalar2=None, op0=ALU.mult
+            )
+            nc.vector.tensor_scalar(
+                out=fine[:, i, :], in0=pos[:], scalar1=turns[i] - coarse_turns[i], scalar2=None, op0=ALU.mult
+            )
+        else:
+            nc.scalar.mul(out=frac[:, 0, i, :], in_=pos[:], mul=turns[i])
 
-    whole = pool.tile([P, PAIRS, TILES], F32)
+    whole = pool.tile([P, fast, TILES], F32)
     nc.vector.tensor_scalar(
         out=whole[:],
         in0=coarse[:],
@@ -83,9 +97,8 @@ def build_rope_versines(nc, pool):
         op0=ALU.add,
         op1=ALU.subtract,
     )
-    frac = pool.tile([P, 3, PAIRS, TILES], F32)
-    nc.vector.tensor_tensor(out=frac[:, 0], in0=coarse[:], in1=whole[:], op=ALU.subtract)
-    nc.vector.tensor_tensor(out=frac[:, 0], in0=frac[:, 0], in1=fine[:], op=ALU.add)
+    nc.vector.tensor_tensor(out=coarse[:], in0=coarse[:], in1=whole[:], op=ALU.subtract)
+    nc.vector.tensor_tensor(out=frac[:, 0, :fast], in0=coarse[:], in1=fine[:], op=ALU.add)
     nc.vector.tensor_scalar(out=frac[:, 1], in0=frac[:, 0], scalar1=0.25, scalar2=None, op0=ALU.add)
     nc.vector.tensor_scalar(out=frac[:, 2], in0=frac[:, 0], scalar1=-0.25, scalar2=None, op0=ALU.add)
 
@@ -121,6 +134,7 @@ def tile_causalselfattentiongqa_pa_t_kernel(tc, x, w_qkv, out_0, out_1, out_2):
     with ExitStack() as ctx:
         const = ctx.enter_context(tc.tile_pool(name="const", bufs=1))
         x_pool = ctx.enter_context(tc.tile_pool(name="x", bufs=ALL_CHUNKS))
+        reorder_pool = ctx.enter_context(tc.tile_pool(name="reorder", bufs=3))
         mx_pool = ctx.enter_context(tc.tile_pool(name="mx", bufs=3))
         rope_pool = ctx.enter_context(tc.tile_pool(name="rope", bufs=3))
         out_pool = ctx.enter_context(tc.tile_pool(name="out", bufs=STORES))
@@ -130,23 +144,33 @@ def tile_causalselfattentiongqa_pa_t_kernel(tc, x, w_qkv, out_0, out_1, out_2):
 
         x_rows = x.rearrange("b (p j) d -> b p (j d)", j=TILES)
         x_chunks = {}
+        reordered_tiles = {}
         mx_tiles = {}
         u_banks = {}
         rope_tiles = {}
         out_tiles = {}
 
-        def load(n, parts):
+        def load(n, parts, begin, end):
             b, c = divmod(n, CHUNKS)
-            x_chunk = x_pool.tile([P, CHUNK_TILES * D_MODEL], BF16)
+            if begin == 0:
+                x_chunk = x_pool.tile([P, CHUNK_TILES * D_MODEL], BF16)
+                x_chunks[n] = x_chunk
+            x_chunk = x_chunks[n]
             width = CHUNK_TILES * D_MODEL // parts
-            for part in range(parts):
+            for part in range(begin, end):
                 lo = part * width
                 first = c * CHUNK_TILES * D_MODEL + lo
                 nc.sync.dma_start(out=x_chunk[:, lo : lo + width], in_=x_rows[b, :, first : first + width])
-            x_chunks[n] = x_chunk
 
-        def transpose_and_quantise(n, half):
-            if half == 0:
+        def reorder(n):
+            reordered = reorder_pool.tile([P, WORD_BLOCKS, P], F32)
+            words = x_chunks[n][:].bitcast(F32)[:, CHUNK_TILES * TILE_WORDS - PASS_WORDS :]
+            nc.scalar.copy(out=reordered[:], in_=words.rearrange("p (w u) -> p u w", u=WORD_BLOCKS))
+            reordered_tiles[n] = reordered
+
+        def transpose(unit):
+            n, lo, hi = unit
+            if lo == 0:
                 grouped = mx_pool.tile([P, CHUNK_TILES * PASSES * P * PACK], BF16, align_bytes=64)
                 codes = mx_pool.tile([P, CHUNK_TILES * PASSES * P], U32, align_bytes=64)
                 scales = mx_pool.tile([P, CHUNK_TILES * PASSES * P], U8, align_bytes=64)
@@ -156,135 +180,189 @@ def tile_causalselfattentiongqa_pa_t_kernel(tc, x, w_qkv, out_0, out_1, out_2):
             grouped_words = grouped[:].bitcast(F32).rearrange(
                 "p (j g c u) -> p j g c u", j=CHUNK_TILES, g=PASSES, u=WORD_BLOCKS
             )
-            for jj in range(half * QUANT_TILES, (half + 1) * QUANT_TILES):
+            for jj in range(lo, hi):
                 xt = psum_t.tile([P, PASSES, WORD_BLOCKS, P], F32)
                 for g in range(PASSES):
                     for u in range(WORD_BLOCKS):
-                        first = (jj * PASSES + g) * WORD_BLOCKS * P
-                        words = x_words[:, first + u : first + WORD_BLOCKS * P : WORD_BLOCKS]
+                        if n in reordered_tiles and jj == CHUNK_TILES - 1 and g == PASSES - 1:
+                            words = reordered_tiles[n][:, u, :]
+                        else:
+                            first = (jj * PASSES + g) * PASS_WORDS
+                            words = x_words[:, first + u : first + PASS_WORDS : WORD_BLOCKS]
                         nc.tensor.transpose(xt[:, g, u, :], words, identity[:])
                 nc.scalar.copy(out=grouped_words[:, jj], in_=xt[:].rearrange("p g u c -> p g c u"))
-            words = QUANT_TILES * PASSES * P
-            lo = half * words
+
+        def quantise(unit):
+            n, lo, hi = unit
+            grouped, codes, scales = mx_tiles[n]
+            words = slice(lo * PASSES * P, hi * PASSES * P)
             nc.vector.quantize_mx(
-                out=codes[:, lo : lo + words].bitcast(FP8X4),
-                scales=scales[:, lo : lo + words],
-                in_=grouped[:, lo * PACK : (lo + words) * PACK],
+                out=codes[:, words].bitcast(FP8X4),
+                scales=scales[:, words],
+                in_=grouped[:, lo * PASSES * P * PACK : hi * PASSES * P * PACK],
             )
 
-        def project(n):
+        def project(unit):
+            n, lo, hi = unit
             grouped, codes, scales = mx_tiles[n]
             u_bank = psum_u.tile([P, CHUNK_TILES, FEATURES], F32)
-            for jj in range(CHUNK_TILES):
+            for jj in range(lo, hi):
                 for g in range(PASSES):
-                    lo = (jj * PASSES + g) * P
+                    first = (jj * PASSES + g) * P
                     nc.tensor.matmul_mx(
                         out=u_bank[:, jj, :],
-                        lhsT=codes[:, lo : lo + P].bitcast(FP8X4),
-                        lhsT_scale=scales[:, lo : lo + P],
+                        lhsT=codes[:, first : first + P].bitcast(FP8X4),
+                        lhsT_scale=scales[:, first : first + P],
                         rhs=w_codes[:, g * FEATURES : (g + 1) * FEATURES].bitcast(FP8X4),
                         rhs_scale=w_scales[:, g * FEATURES : (g + 1) * FEATURES],
                         start=(g == 0),
                         stop=(g == PASSES - 1),
                     )
-            u_banks[n] = u_bank
+            u_banks[unit] = u_bank
 
-        def rope_products(n):
+        def rope_products(unit):
+            n, lo, hi = unit
+            tiles = hi - lo
             c = n % CHUNKS
-            if c % STORE_CHUNKS == 0:
+            if c % STORE_CHUNKS == 0 and lo == 0:
                 out_sb = out_pool.tile([P, HEADS, STORE_TILES, HEAD_DIM], F32)
                 out_tiles[n // STORE_CHUNKS] = out_sb
             out_sb = out_tiles[n // STORE_CHUNKS]
-            u_bank = u_banks[n]
-            j_batch = c * CHUNK_TILES
-            j_store = (c % STORE_CHUNKS) * CHUNK_TILES
+            u_bank = u_banks[unit]
+            j_batch = c * CHUNK_TILES + lo
+            j_store = (c % STORE_CHUNKS) * CHUNK_TILES + lo
             nc.scalar.copy(
-                out=out_sb[:, ROPE_HEADS, j_store : j_store + CHUNK_TILES, :],
-                in_=u_bank[:, :, ROPE_COLS:],
+                out=out_sb[:, ROPE_HEADS, j_store : j_store + tiles, :],
+                in_=u_bank[:, lo:hi, ROPE_COLS:],
             )
-            roped = u_bank[:, :, :ROPE_COLS]
-            by_cos = rope_pool.tile([P, CHUNK_TILES, ROPE_HEADS, HEAD_DIM], F32)
+            roped = u_bank[:, lo:hi, :ROPE_COLS]
+            by_cos = rope_pool.tile([P, tiles, ROPE_HEADS, HEAD_DIM], F32)
             nc.vector.tensor_tensor(
                 out=by_cos[:],
                 in0=roped.rearrange("p j (h d) -> p j h d", h=ROPE_HEADS),
-                in1=cos_tab[:, j_batch : j_batch + CHUNK_TILES]
+                in1=cos_tab[:, j_batch : j_batch + tiles]
                 .rearrange("p j i two -> p j (i two)")
                 .unsqueeze(2)
-                .to_broadcast([P, CHUNK_TILES, ROPE_HEADS, HEAD_DIM]),
+                .to_broadcast([P, tiles, ROPE_HEADS, HEAD_DIM]),
                 op=ALU.mult,
             )
-            by_sin = rope_pool.tile([P, CHUNK_TILES, ROPE_HEADS, PAIRS, 2], F32)
+            by_sin = rope_pool.tile([P, tiles, ROPE_HEADS, PAIRS, 2], F32)
             nc.vector.tensor_tensor(
                 out=by_sin[:],
                 in0=roped.rearrange("p j (h i two) -> p j h i two", h=ROPE_HEADS, two=2)[:, :, :, :, ::-1],
-                in1=sin_tab[:, j_batch : j_batch + CHUNK_TILES]
+                in1=sin_tab[:, j_batch : j_batch + tiles]
                 .unsqueeze(2)
-                .to_broadcast([P, CHUNK_TILES, ROPE_HEADS, PAIRS, 2]),
+                .to_broadcast([P, tiles, ROPE_HEADS, PAIRS, 2]),
                 op=ALU.mult,
             )
-            rope_tiles[n] = (by_cos, by_sin)
+            rope_tiles[unit] = (by_cos, by_sin)
 
-        def rope_sum_and_store(n):
-            b, c = divmod(n, CHUNKS)
+        def rope_sum(unit):
+            n, lo, hi = unit
             out_sb = out_tiles[n // STORE_CHUNKS]
-            by_cos, by_sin = rope_tiles[n]
-            j_store = (c % STORE_CHUNKS) * CHUNK_TILES
+            by_cos, by_sin = rope_tiles[unit]
+            j_store = (n % STORE_CHUNKS) * CHUNK_TILES + lo
             nc.vector.tensor_tensor(
-                out=out_sb[:, :ROPE_HEADS, j_store : j_store + CHUNK_TILES, :].rearrange("p h j d -> p j h d"),
+                out=out_sb[:, :ROPE_HEADS, j_store : j_store + hi - lo, :].rearrange("p h j d -> p j h d"),
                 in0=by_cos[:],
                 in1=by_sin[:].rearrange("p j h i two -> p j h (i two)"),
                 op=ALU.add,
             )
-            if c % STORE_CHUNKS == STORE_CHUNKS - 1:
-                j0 = (c + 1) * CHUNK_TILES - STORE_TILES
-                nc.sync.dma_start(
-                    out=out_0[b, 0].rearrange("h (p j) d -> p h j d", j=TILES)[:, :, j0 : j0 + STORE_TILES, :],
-                    in_=out_sb[:, 0:2],
-                )
-                nc.sync.dma_start(
-                    out=out_1[b, 0].rearrange("(p j) d -> p j d", j=TILES)[:, j0 : j0 + STORE_TILES, :],
-                    in_=out_sb[:, 2],
-                )
-                nc.sync.dma_start(
-                    out=out_2[b, 0].rearrange("(p j) d -> p j d", j=TILES)[:, j0 : j0 + STORE_TILES, :],
-                    in_=out_sb[:, 3],
-                )
 
-        load(0, HALVES)
+        def store(n, chunks):
+            b, c = divmod(n, CHUNKS)
+            out_sb = out_tiles[n // STORE_CHUNKS]
+            tiles = chunks * CHUNK_TILES
+            j_batch = (c + 1) * CHUNK_TILES - tiles
+            j_store = (c % STORE_CHUNKS + 1) * CHUNK_TILES - tiles
+            in_batch = slice(j_batch, j_batch + tiles)
+            in_store = slice(j_store, j_store + tiles)
+            nc.sync.dma_start(
+                out=out_0[b, 0].rearrange("h (p j) d -> p h j d", j=TILES)[:, :, in_batch, :],
+                in_=out_sb[:, 0:2, in_store],
+            )
+            nc.sync.dma_start(
+                out=out_1[b, 0].rearrange("(p j) d -> p j d", j=TILES)[:, in_batch, :],
+                in_=out_sb[:, 2, in_store],
+            )
+            nc.sync.dma_start(
+                out=out_2[b, 0].rearrange("(p j) d -> p j d", j=TILES)[:, in_batch, :],
+                in_=out_sb[:, 3, in_store],
+            )
+
+        load(0, CHUNK_TILES, 0, CHUNK_TILES)
+        load(1, HALVES, 0, 1)
         w_raw = const.tile([P, PASSES, PACK, FEATURES], BF16)
         nc.sync.dma_start(
             out=w_raw[:].rearrange("p g t c -> p g (t c)"),
             in_=w_qkv.rearrange("(g p t) c -> p g (t c)", p=P, t=PACK),
         )
-        for n in range(1, ALL_CHUNKS):
-            load(n, 1)
+        load(1, HALVES, 1, HALVES)
+        for n in range(2, ALL_CHUNKS):
+            parts = HALVES if n < EARLY_CHUNKS else 1
+            load(n, parts, 0, parts)
 
-        versine = build_rope_versines(nc, const)
+        pos = build_positions(nc, const)
+        versine = build_rope_versines(nc, const, pos)
+        cos_tab = const.tile([P, TILES, PAIRS, 2], F32)
+        sin_tab = const.tile([P, TILES, PAIRS, 2], F32)
+        finish_rope_tables(nc, versine, cos_tab, sin_tab)
 
         identity = const.tile([P, P], F32)
         make_identity(nc, identity[:])
 
         w_grouped = const.tile([P, PASSES, FEATURES, PACK], BF16, align_bytes=64)
-        nc.vector.tensor_copy(out=w_grouped[:], in_=w_raw[:].rearrange("p g t c -> p g c t"))
         w_codes = const.tile([P, PASSES * FEATURES], U32, align_bytes=64)
         w_scales = const.tile([P, PASSES * FEATURES], U8, align_bytes=64)
-        nc.vector.quantize_mx(
-            out=w_codes[:].bitcast(FP8X4),
-            scales=w_scales[:],
-            in_=w_grouped[:].rearrange("p g c t -> p (g c t)"),
-        )
 
-        cos_tab = const.tile([P, TILES, PAIRS, 2], F32)
-        sin_tab = const.tile([P, TILES, PAIRS, 2], F32)
-        finish_rope_tables(nc, versine, cos_tab, sin_tab)
+        def quantise_weights():
+            nc.vector.tensor_copy(out=w_grouped[:], in_=w_raw[:].rearrange("p g t c -> p g c t"))
+            nc.vector.quantize_mx(
+                out=w_codes[:].bitcast(FP8X4),
+                scales=w_scales[:],
+                in_=w_grouped[:].rearrange("p g c t -> p (g c t)"),
+            )
 
-        for n in range(ALL_CHUNKS + 2):
-            if n < ALL_CHUNKS:
-                transpose_and_quantise(n, 0)
+        def whole(n):
+            return (n, 0, CHUNK_TILES)
+
+        def first_half(n):
+            return (n, 0, HALF_TILES)
+
+        def second_half(n):
+            return (n, HALF_TILES, CHUNK_TILES)
+
+        last = ALL_CHUNKS - 1
+        for n in range(last):
+            transpose(first_half(n))
+            quantise(first_half(n))
             if 0 <= n - 2:
-                rope_sum_and_store(n - 2)
-            if n < ALL_CHUNKS:
-                transpose_and_quantise(n, 1)
-            if 0 <= n - 1 < ALL_CHUNKS:
-                project(n - 1)
-                rope_products(n - 1)
+                rope_sum(whole(n - 2))
+                if (n - 2) % STORE_CHUNKS == STORE_CHUNKS - 1:
+                    store(n - 2, STORE_CHUNKS)
+            transpose(second_half(n))
+            quantise(second_half(n))
+            reorder(n + 1)
+            if n == 0:
+                quantise_weights()
+            if 0 <= n - 1:
+                project(whole(n - 1))
+                rope_products(whole(n - 1))
+
+        transpose(first_half(last))
+        quantise(first_half(last))
+        rope_sum(whole(last - 2))
+        store(last - 2, STORE_CHUNKS)
+        project(whole(last - 1))
+        rope_products(whole(last - 1))
+        transpose(second_half(last))
+        quantise(second_half(last))
+        project(first_half(last))
+        rope_products(first_half(last))
+        rope_sum(whole(last - 1))
+        store(last - 1, 1)
+        project(second_half(last))
+        rope_products(second_half(last))
+        rope_sum(first_half(last))
+        rope_sum(second_half(last))
+        store(last, 1)

@@ -39,7 +39,9 @@ STORE_CHUNKS = 2
 STORE_TILES = STORE_CHUNKS * CHUNK_TILES
 ALL_CHUNKS = BATCH * CHUNKS
 HALVES = 2
-EARLY_CHUNKS = 5
+EARLY_CHUNKS = 4
+FIRST_REORDERED = 3
+REORDERED_TILE = CHUNK_TILES - 1
 STORES = ALL_CHUNKS // STORE_CHUNKS
 
 ROPE_THETA = 1e6
@@ -67,7 +69,7 @@ def build_positions(nc, pool):
     return pos
 
 
-def build_rope_versines(nc, pool, pos):
+def build_rope_squares(nc, pool, pos):
     sin_first = pool.tile([P, 1], F32)
     nc.scalar.activation(out=sin_first[:], in_=pos[:, 0:1], func=ACT.Sin, scale=0.0)
 
@@ -99,30 +101,32 @@ def build_rope_versines(nc, pool, pos):
     )
     nc.vector.tensor_tensor(out=coarse[:], in0=coarse[:], in1=whole[:], op=ALU.subtract)
     nc.vector.tensor_tensor(out=frac[:, 0, :fast], in0=coarse[:], in1=fine[:], op=ALU.add)
-    nc.vector.tensor_scalar(out=frac[:, 1], in0=frac[:, 0], scalar1=0.25, scalar2=None, op0=ALU.add)
-    nc.vector.tensor_scalar(out=frac[:, 2], in0=frac[:, 0], scalar1=-0.25, scalar2=None, op0=ALU.add)
+    nc.vector.tensor_scalar(out=frac[:, 1], in0=frac[:, 0], scalar1=-0.25, scalar2=None, op0=ALU.add)
+    nc.vector.tensor_scalar(out=frac[:, 2], in0=frac[:, 0], scalar1=0.25, scalar2=None, op0=ALU.add)
 
-    versine = pool.tile([P, 3, PAIRS, TILES], F32)
-    nc.scalar.activation(out=versine[:], in_=frac[:], func=ACT.Sin, scale=math.pi)
-    nc.scalar.activation(
-        out=versine[:], in_=versine[:], func=ACT.Square, scale=math.sqrt(2.0 * ATTN_FACTOR)
-    )
-    return versine
+    half_sine = pool.tile([P, 3, PAIRS, TILES], F32)
+    nc.scalar.activation(out=half_sine[:], in_=frac[:], func=ACT.Sin, scale=math.pi)
+    square = pool.tile([P, 3, PAIRS, TILES], F32)
+    nc.vector.tensor_tensor(out=square[:], in0=half_sine[:], in1=half_sine[:], op=ALU.mult)
+    return square
 
 
-def finish_rope_tables(nc, versine, cos_tab, sin_tab):
+def finish_rope_tables(nc, square, table):
     nc.vector.tensor_scalar(
-        out=cos_tab[:],
-        in0=versine[:, 0].rearrange("p i j -> p j i").unsqueeze(3).to_broadcast([P, TILES, PAIRS, 2]),
-        scalar1=-1.0,
+        out=table[:, :, 0].rearrange("p n j (i e) -> p n j i e", e=2),
+        in0=square[:, 0]
+        .rearrange("p i (n j) -> p n j i", j=CHUNK_TILES)
+        .unsqueeze(4)
+        .to_broadcast([P, CHUNKS, CHUNK_TILES, PAIRS, 2]),
+        scalar1=-2.0 * ATTN_FACTOR,
         scalar2=ATTN_FACTOR,
         op0=ALU.mult,
         op1=ALU.add,
     )
     nc.vector.tensor_scalar(
-        out=sin_tab[:],
-        in0=versine[:, 1:3].rearrange("p s i j -> p j i s"),
-        scalar1=-1.0,
+        out=table[:, :, 1].rearrange("p n j (i e) -> p n j i e", e=2),
+        in0=square[:, 1:3].rearrange("p e i (n j) -> p n j i e", j=CHUNK_TILES),
+        scalar1=-2.0 * ATTN_FACTOR,
         scalar2=ATTN_FACTOR,
         op0=ALU.mult,
         op1=ALU.add,
@@ -134,7 +138,7 @@ def tile_causalselfattentiongqa_pa_t_kernel(tc, x, w_qkv, out_0, out_1, out_2):
     with ExitStack() as ctx:
         const = ctx.enter_context(tc.tile_pool(name="const", bufs=1))
         x_pool = ctx.enter_context(tc.tile_pool(name="x", bufs=ALL_CHUNKS))
-        reorder_pool = ctx.enter_context(tc.tile_pool(name="reorder", bufs=3))
+        reorder_pool = ctx.enter_context(tc.tile_pool(name="reorder", bufs=4))
         mx_pool = ctx.enter_context(tc.tile_pool(name="mx", bufs=3))
         rope_pool = ctx.enter_context(tc.tile_pool(name="rope", bufs=3))
         out_pool = ctx.enter_context(tc.tile_pool(name="out", bufs=STORES))
@@ -162,11 +166,13 @@ def tile_causalselfattentiongqa_pa_t_kernel(tc, x, w_qkv, out_0, out_1, out_2):
                 first = c * CHUNK_TILES * D_MODEL + lo
                 nc.sync.dma_start(out=x_chunk[:, lo : lo + width], in_=x_rows[b, :, first : first + width])
 
-        def reorder(n):
-            reordered = reorder_pool.tile([P, WORD_BLOCKS, P], F32)
-            words = x_chunks[n][:].bitcast(F32)[:, CHUNK_TILES * TILE_WORDS - PASS_WORDS :]
-            nc.scalar.copy(out=reordered[:], in_=words.rearrange("p (w u) -> p u w", u=WORD_BLOCKS))
-            reordered_tiles[n] = reordered
+        def reorder(n, g, copy):
+            if FIRST_REORDERED <= n < ALL_CHUNKS:
+                reordered = reorder_pool.tile([P, WORD_BLOCKS, P], F32)
+                first = (REORDERED_TILE * PASSES + g) * PASS_WORDS
+                words = x_chunks[n][:].bitcast(F32)[:, first : first + PASS_WORDS]
+                copy(out=reordered[:], in_=words.rearrange("p (w u) -> p u w", u=WORD_BLOCKS))
+                reordered_tiles[n, g] = reordered
 
         def transpose(unit):
             n, lo, hi = unit
@@ -184,8 +190,8 @@ def tile_causalselfattentiongqa_pa_t_kernel(tc, x, w_qkv, out_0, out_1, out_2):
                 xt = psum_t.tile([P, PASSES, WORD_BLOCKS, P], F32)
                 for g in range(PASSES):
                     for u in range(WORD_BLOCKS):
-                        if n in reordered_tiles and jj == CHUNK_TILES - 1 and g == PASSES - 1:
-                            words = reordered_tiles[n][:, u, :]
+                        if jj == REORDERED_TILE and n >= FIRST_REORDERED:
+                            words = reordered_tiles[n, g][:, u, :]
                         else:
                             first = (jj * PASSES + g) * PASS_WORDS
                             words = x_words[:, first + u : first + PASS_WORDS : WORD_BLOCKS]
@@ -229,84 +235,79 @@ def tile_causalselfattentiongqa_pa_t_kernel(tc, x, w_qkv, out_0, out_1, out_2):
                 out_tiles[n // STORE_CHUNKS] = out_sb
             out_sb = out_tiles[n // STORE_CHUNKS]
             u_bank = u_banks[unit]
-            j_batch = c * CHUNK_TILES + lo
             j_store = (c % STORE_CHUNKS) * CHUNK_TILES + lo
             nc.scalar.copy(
                 out=out_sb[:, ROPE_HEADS, j_store : j_store + tiles, :],
                 in_=u_bank[:, lo:hi, ROPE_COLS:],
             )
-            roped = u_bank[:, lo:hi, :ROPE_COLS]
-            by_cos = rope_pool.tile([P, tiles, ROPE_HEADS, HEAD_DIM], F32)
-            nc.vector.tensor_tensor(
-                out=by_cos[:],
-                in0=roped.rearrange("p j (h d) -> p j h d", h=ROPE_HEADS),
-                in1=cos_tab[:, j_batch : j_batch + tiles]
-                .rearrange("p j i two -> p j (i two)")
-                .unsqueeze(2)
-                .to_broadcast([P, tiles, ROPE_HEADS, HEAD_DIM]),
-                op=ALU.mult,
-            )
-            by_sin = rope_pool.tile([P, tiles, ROPE_HEADS, PAIRS, 2], F32)
-            nc.vector.tensor_tensor(
-                out=by_sin[:],
-                in0=roped.rearrange("p j (h i two) -> p j h i two", h=ROPE_HEADS, two=2)[:, :, :, :, ::-1],
-                in1=sin_tab[:, j_batch : j_batch + tiles]
-                .unsqueeze(2)
-                .to_broadcast([P, tiles, ROPE_HEADS, PAIRS, 2]),
-                op=ALU.mult,
-            )
-            rope_tiles[unit] = (by_cos, by_sin)
+            products = rope_pool.tile([P, 2, tiles, ROPE_COLS], F32)
+            roped = u_bank[:, lo:hi, :ROPE_COLS].rearrange("p j (h d) -> p j h d", h=ROPE_HEADS)
+            if tiles == CHUNK_TILES:
+                both = [P, 2, tiles, ROPE_HEADS, HEAD_DIM]
+                nc.vector.tensor_tensor(
+                    out=products[:].rearrange("p s j (h d) -> p s j h d", h=ROPE_HEADS),
+                    in0=roped.unsqueeze(1).to_broadcast(both),
+                    in1=table[:, c].unsqueeze(3).to_broadcast(both),
+                    op=ALU.mult,
+                )
+            else:
+                for s in range(2):
+                    nc.vector.tensor_tensor(
+                        out=products[:, s].rearrange("p j (h d) -> p j h d", h=ROPE_HEADS),
+                        in0=roped,
+                        in1=table[:, c, s, lo:hi].unsqueeze(2).to_broadcast([P, tiles, ROPE_HEADS, HEAD_DIM]),
+                        op=ALU.mult,
+                    )
+            rope_tiles[unit] = products
 
-        def rope_sum(unit):
+        def rope_sum(unit, engine=nc.vector):
             n, lo, hi = unit
             out_sb = out_tiles[n // STORE_CHUNKS]
-            by_cos, by_sin = rope_tiles[unit]
+            products = rope_tiles[unit]
             j_store = (n % STORE_CHUNKS) * CHUNK_TILES + lo
-            nc.vector.tensor_tensor(
-                out=out_sb[:, :ROPE_HEADS, j_store : j_store + hi - lo, :].rearrange("p h j d -> p j h d"),
-                in0=by_cos[:],
-                in1=by_sin[:].rearrange("p j h i two -> p j h (i two)"),
+            pairs = "p j (h i e) -> p j h i e"
+            engine.tensor_tensor(
+                out=out_sb[:, :ROPE_HEADS, j_store : j_store + hi - lo, :].rearrange(
+                    "p h j (i e) -> p j h i e", e=2
+                ),
+                in0=products[:, 0].rearrange(pairs, h=ROPE_HEADS, e=2),
+                in1=products[:, 1].rearrange(pairs, h=ROPE_HEADS, e=2)[:, :, :, :, ::-1],
                 op=ALU.add,
             )
 
-        def store(n, chunks):
+        def store(n, lo, hi):
             b, c = divmod(n, CHUNKS)
             out_sb = out_tiles[n // STORE_CHUNKS]
-            tiles = chunks * CHUNK_TILES
-            j_batch = (c + 1) * CHUNK_TILES - tiles
-            j_store = (c % STORE_CHUNKS + 1) * CHUNK_TILES - tiles
-            in_batch = slice(j_batch, j_batch + tiles)
-            in_store = slice(j_store, j_store + tiles)
+            in_batch = slice(c * CHUNK_TILES + lo, c * CHUNK_TILES + hi)
+            nc.sync.dma_start(
+                out=out_2[b, 0].rearrange("(p j) d -> p j d", j=TILES)[:, in_batch, :],
+                in_=out_sb[:, 3, lo:hi],
+            )
             nc.sync.dma_start(
                 out=out_0[b, 0].rearrange("h (p j) d -> p h j d", j=TILES)[:, :, in_batch, :],
-                in_=out_sb[:, 0:2, in_store],
+                in_=out_sb[:, 0:2, lo:hi],
             )
             nc.sync.dma_start(
                 out=out_1[b, 0].rearrange("(p j) d -> p j d", j=TILES)[:, in_batch, :],
-                in_=out_sb[:, 2, in_store],
-            )
-            nc.sync.dma_start(
-                out=out_2[b, 0].rearrange("(p j) d -> p j d", j=TILES)[:, in_batch, :],
-                in_=out_sb[:, 3, in_store],
+                in_=out_sb[:, 2, lo:hi],
             )
 
         load(0, CHUNK_TILES, 0, CHUNK_TILES)
-        load(1, HALVES, 0, 1)
+        load(1, CHUNK_TILES, 0, HALF_TILES)
         w_raw = const.tile([P, PASSES, PACK, FEATURES], BF16)
         nc.sync.dma_start(
             out=w_raw[:].rearrange("p g t c -> p g (t c)"),
             in_=w_qkv.rearrange("(g p t) c -> p g (t c)", p=P, t=PACK),
         )
-        load(1, HALVES, 1, HALVES)
+        load(1, CHUNK_TILES, HALF_TILES, CHUNK_TILES)
         for n in range(2, ALL_CHUNKS):
             parts = HALVES if n < EARLY_CHUNKS else 1
             load(n, parts, 0, parts)
 
         pos = build_positions(nc, const)
-        versine = build_rope_versines(nc, const, pos)
-        cos_tab = const.tile([P, TILES, PAIRS, 2], F32)
-        sin_tab = const.tile([P, TILES, PAIRS, 2], F32)
-        finish_rope_tables(nc, versine, cos_tab, sin_tab)
+        square = build_rope_squares(nc, const, pos)
+        table = const.tile([P, CHUNKS, 2, CHUNK_TILES, HEAD_DIM], F32)
+        finish_rope_tables(nc, square, table)
 
         identity = const.tile([P, P], F32)
         make_identity(nc, identity[:])
@@ -339,30 +340,31 @@ def tile_causalselfattentiongqa_pa_t_kernel(tc, x, w_qkv, out_0, out_1, out_2):
             if 0 <= n - 2:
                 rope_sum(whole(n - 2))
                 if (n - 2) % STORE_CHUNKS == STORE_CHUNKS - 1:
-                    store(n - 2, STORE_CHUNKS)
+                    store(n - 1 - STORE_CHUNKS, 0, STORE_TILES)
             transpose(second_half(n))
             quantise(second_half(n))
-            reorder(n + 1)
+            reorder(n + 1, 1, nc.scalar.copy)
             if n == 0:
                 quantise_weights()
             if 0 <= n - 1:
                 project(whole(n - 1))
                 rope_products(whole(n - 1))
+            reorder(n + 2, 0, nc.vector.tensor_copy)
 
         transpose(first_half(last))
         quantise(first_half(last))
         rope_sum(whole(last - 2))
-        store(last - 2, STORE_CHUNKS)
-        project(whole(last - 1))
-        rope_products(whole(last - 1))
+        store(last - 3, 0, STORE_TILES)
         transpose(second_half(last))
+        project(whole(last - 1))
         quantise(second_half(last))
+        rope_products(whole(last - 1))
         project(first_half(last))
         rope_products(first_half(last))
-        rope_sum(whole(last - 1))
-        store(last - 1, 1)
+        rope_sum(whole(last - 1), nc.gpsimd)
+        store(last - 1, 0, CHUNK_TILES)
         project(second_half(last))
         rope_products(second_half(last))
         rope_sum(first_half(last))
         rope_sum(second_half(last))
-        store(last, 1)
+        store(last - 1, CHUNK_TILES, STORE_TILES)

@@ -22,6 +22,8 @@ PAIRS = HEAD_DIM // 2
 ROPE_HEADS = 3
 HEADS = 4
 FEATURES = HEADS * HEAD_DIM
+QUERY_HEADS = (0, 2)
+KEY_HEAD = (2, 3)
 ROPE_COLS = ROPE_HEADS * HEAD_DIM
 
 PACK = 4
@@ -138,7 +140,7 @@ def tile_causalselfattentiongqa_pa_t_kernel(tc, x, w_qkv, out_0, out_1, out_2):
     with ExitStack() as ctx:
         const = ctx.enter_context(tc.tile_pool(name="const", bufs=1))
         x_pool = ctx.enter_context(tc.tile_pool(name="x", bufs=ALL_CHUNKS))
-        reorder_pool = ctx.enter_context(tc.tile_pool(name="reorder", bufs=4))
+        reorder_pool = ctx.enter_context(tc.tile_pool(name="reorder", bufs=3))
         mx_pool = ctx.enter_context(tc.tile_pool(name="mx", bufs=3))
         rope_pool = ctx.enter_context(tc.tile_pool(name="rope", bufs=3))
         out_pool = ctx.enter_context(tc.tile_pool(name="out", bufs=STORES))
@@ -166,13 +168,15 @@ def tile_causalselfattentiongqa_pa_t_kernel(tc, x, w_qkv, out_0, out_1, out_2):
                 first = c * CHUNK_TILES * D_MODEL + lo
                 nc.sync.dma_start(out=x_chunk[:, lo : lo + width], in_=x_rows[b, :, first : first + width])
 
-        def reorder(n, g, copy):
+        def reorder(n):
             if FIRST_REORDERED <= n < ALL_CHUNKS:
-                reordered = reorder_pool.tile([P, WORD_BLOCKS, P], F32)
-                first = (REORDERED_TILE * PASSES + g) * PASS_WORDS
-                words = x_chunks[n][:].bitcast(F32)[:, first : first + PASS_WORDS]
-                copy(out=reordered[:], in_=words.rearrange("p (w u) -> p u w", u=WORD_BLOCKS))
-                reordered_tiles[n, g] = reordered
+                reordered = reorder_pool.tile([P, PASSES, WORD_BLOCKS, P], F32)
+                first = REORDERED_TILE * TILE_WORDS
+                words = x_chunks[n][:].bitcast(F32)[:, first : first + TILE_WORDS]
+                nc.vector.tensor_copy(
+                    out=reordered[:], in_=words.rearrange("p (g w u) -> p g u w", g=PASSES, u=WORD_BLOCKS)
+                )
+                reordered_tiles[n] = reordered
 
         def transpose(unit):
             n, lo, hi = unit
@@ -191,7 +195,7 @@ def tile_causalselfattentiongqa_pa_t_kernel(tc, x, w_qkv, out_0, out_1, out_2):
                 for g in range(PASSES):
                     for u in range(WORD_BLOCKS):
                         if jj == REORDERED_TILE and n >= FIRST_REORDERED:
-                            words = reordered_tiles[n, g][:, u, :]
+                            words = reordered_tiles[n][:, g, u, :]
                         else:
                             first = (jj * PASSES + g) * PASS_WORDS
                             words = x_words[:, first + u : first + PASS_WORDS : WORD_BLOCKS]
@@ -260,18 +264,23 @@ def tile_causalselfattentiongqa_pa_t_kernel(tc, x, w_qkv, out_0, out_1, out_2):
                     )
             rope_tiles[unit] = products
 
-        def rope_sum(unit, engine=nc.vector):
+        def hold_sum(n):
+            j_store = (n % STORE_CHUNKS) * CHUNK_TILES
+            nc.vector.memset(out_tiles[n // STORE_CHUNKS][:, 0, j_store, 0:1], 0.0)
+
+        def rope_sum(unit, engine=nc.vector, heads=(0, ROPE_HEADS)):
             n, lo, hi = unit
             out_sb = out_tiles[n // STORE_CHUNKS]
             products = rope_tiles[unit]
             j_store = (n % STORE_CHUNKS) * CHUNK_TILES + lo
-            pairs = "p j (h i e) -> p j h i e"
+            begin, end = heads
+            pairs = products[:].rearrange("p s j (h i e) -> p s j h i e", h=ROPE_HEADS, e=2)
             engine.tensor_tensor(
-                out=out_sb[:, :ROPE_HEADS, j_store : j_store + hi - lo, :].rearrange(
+                out=out_sb[:, begin:end, j_store : j_store + hi - lo, :].rearrange(
                     "p h j (i e) -> p j h i e", e=2
                 ),
-                in0=products[:, 0].rearrange(pairs, h=ROPE_HEADS, e=2),
-                in1=products[:, 1].rearrange(pairs, h=ROPE_HEADS, e=2)[:, :, :, :, ::-1],
+                in0=pairs[:, 0, :, begin:end],
+                in1=pairs[:, 1, :, begin:end, :, ::-1],
                 op=ALU.add,
             )
 
@@ -338,27 +347,32 @@ def tile_causalselfattentiongqa_pa_t_kernel(tc, x, w_qkv, out_0, out_1, out_2):
             transpose(first_half(n))
             quantise(first_half(n))
             if 0 <= n - 2:
-                rope_sum(whole(n - 2))
-                if (n - 2) % STORE_CHUNKS == STORE_CHUNKS - 1:
-                    store(n - 1 - STORE_CHUNKS, 0, STORE_TILES)
+                rope_sum(whole(n - 2), nc.vector, KEY_HEAD)
             transpose(second_half(n))
             quantise(second_half(n))
-            reorder(n + 1, 1, nc.scalar.copy)
+            if 0 <= n - 2:
+                hold_sum(n - 2)
             if n == 0:
                 quantise_weights()
             if 0 <= n - 1:
                 project(whole(n - 1))
                 rope_products(whole(n - 1))
-            reorder(n + 2, 0, nc.vector.tensor_copy)
+            if 0 <= n - 2:
+                rope_sum(whole(n - 2), nc.gpsimd, QUERY_HEADS)
+                if (n - 2) % STORE_CHUNKS == STORE_CHUNKS - 1:
+                    store(n - 1 - STORE_CHUNKS, 0, STORE_TILES)
+            reorder(n + 2)
 
         transpose(first_half(last))
         quantise(first_half(last))
-        rope_sum(whole(last - 2))
-        store(last - 3, 0, STORE_TILES)
+        rope_sum(whole(last - 2), nc.vector, KEY_HEAD)
         transpose(second_half(last))
         project(whole(last - 1))
         quantise(second_half(last))
+        hold_sum(last - 2)
         rope_products(whole(last - 1))
+        rope_sum(whole(last - 2), nc.gpsimd, QUERY_HEADS)
+        store(last - 3, 0, STORE_TILES)
         project(first_half(last))
         rope_products(first_half(last))
         rope_sum(whole(last - 1), nc.gpsimd)

@@ -22,8 +22,6 @@ PAIRS = HEAD_DIM // 2
 ROPE_HEADS = 3
 HEADS = 4
 FEATURES = HEADS * HEAD_DIM
-QUERY_HEADS = (0, 2)
-KEY_HEAD = (2, 3)
 ROPE_COLS = ROPE_HEADS * HEAD_DIM
 
 PACK = 4
@@ -264,23 +262,26 @@ def tile_causalselfattentiongqa_pa_t_kernel(tc, x, w_qkv, out_0, out_1, out_2):
                     )
             rope_tiles[unit] = products
 
-        def hold_sum(n):
+        def hold_sum(n, transposed):
+            grouped, codes, scales = mx_tiles[transposed]
             j_store = (n % STORE_CHUNKS) * CHUNK_TILES
-            nc.vector.memset(out_tiles[n // STORE_CHUNKS][:, 0, j_store, 0:1], 0.0)
+            width = CHUNK_TILES * PASSES * P * PACK
+            nc.vector.tensor_copy(
+                out=out_tiles[n // STORE_CHUNKS][:, 0, j_store, 0:1], in_=grouped[:, width - 1 : width]
+            )
 
-        def rope_sum(unit, engine=nc.vector, heads=(0, ROPE_HEADS)):
+        def rope_sum(unit, engine=nc.vector):
             n, lo, hi = unit
             out_sb = out_tiles[n // STORE_CHUNKS]
             products = rope_tiles[unit]
             j_store = (n % STORE_CHUNKS) * CHUNK_TILES + lo
-            begin, end = heads
             pairs = products[:].rearrange("p s j (h i e) -> p s j h i e", h=ROPE_HEADS, e=2)
             engine.tensor_tensor(
-                out=out_sb[:, begin:end, j_store : j_store + hi - lo, :].rearrange(
+                out=out_sb[:, :ROPE_HEADS, j_store : j_store + hi - lo, :].rearrange(
                     "p h j (i e) -> p j h i e", e=2
                 ),
-                in0=pairs[:, 0, :, begin:end],
-                in1=pairs[:, 1, :, begin:end, :, ::-1],
+                in0=pairs[:, 0],
+                in1=pairs[:, 1, :, :, :, ::-1],
                 op=ALU.add,
             )
 
@@ -346,32 +347,29 @@ def tile_causalselfattentiongqa_pa_t_kernel(tc, x, w_qkv, out_0, out_1, out_2):
         for n in range(last):
             transpose(first_half(n))
             quantise(first_half(n))
-            if 0 <= n - 2:
-                rope_sum(whole(n - 2), nc.vector, KEY_HEAD)
             transpose(second_half(n))
-            quantise(second_half(n))
             if 0 <= n - 2:
-                hold_sum(n - 2)
+                hold_sum(n - 2, n)
+            quantise(second_half(n))
             if n == 0:
                 quantise_weights()
             if 0 <= n - 1:
                 project(whole(n - 1))
                 rope_products(whole(n - 1))
             if 0 <= n - 2:
-                rope_sum(whole(n - 2), nc.gpsimd, QUERY_HEADS)
+                rope_sum(whole(n - 2), nc.gpsimd)
                 if (n - 2) % STORE_CHUNKS == STORE_CHUNKS - 1:
                     store(n - 1 - STORE_CHUNKS, 0, STORE_TILES)
             reorder(n + 2)
 
         transpose(first_half(last))
         quantise(first_half(last))
-        rope_sum(whole(last - 2), nc.vector, KEY_HEAD)
         transpose(second_half(last))
         project(whole(last - 1))
+        hold_sum(last - 2, last)
         quantise(second_half(last))
-        hold_sum(last - 2)
         rope_products(whole(last - 1))
-        rope_sum(whole(last - 2), nc.gpsimd, QUERY_HEADS)
+        rope_sum(whole(last - 2), nc.gpsimd)
         store(last - 3, 0, STORE_TILES)
         project(first_half(last))
         rope_products(first_half(last))

import math
from contextlib import ExitStack

import concourse.mybir as mybir
from concourse.masks import make_identity

F32 = mybir.dt.float32
BF16 = mybir.dt.bfloat16
I32 = mybir.dt.int32
U32 = mybir.dt.uint32
U8 = mybir.dt.uint8
FP8X4 = mybir.dt.float8_e4m3fn_x4
ALU = mybir.AluOpType
ACT = mybir.ActivationFunctionType

P = 128
BATCH = 4
SEQ = 2048
D_MODEL = 1024
HEAD_DIM = 32
PAIRS = HEAD_DIM // 2
ROPE_HEADS = 3
HEADS = 4
FEATURES = HEADS * HEAD_DIM
ROPE_COLS = ROPE_HEADS * HEAD_DIM

PACK = 4
K_PASS = P * PACK
PASSES = D_MODEL // K_PASS
WORD_BLOCKS = 2

TILES = SEQ // P
CHUNK_TILES = 4
CHUNKS = TILES // CHUNK_TILES
HALF_TILES = CHUNK_TILES // 2
PASS_WORDS = WORD_BLOCKS * P
TILE_WORDS = PASSES * PASS_WORDS
STORE_CHUNKS = 2
STORE_TILES = STORE_CHUNKS * CHUNK_TILES
ALL_CHUNKS = BATCH * CHUNKS
HALVES = 2
EARLY_CHUNKS = 4
FIRST_REORDERED = 3
REORDERED_TILE = CHUNK_TILES - 1
STORES = ALL_CHUNKS // STORE_CHUNKS

ROPE_THETA = 1e6
YARN_FACTOR = 64.0
RAMP_LOW = 5.0
RAMP_HIGH = 8.0
ATTN_FACTOR = 0.1 * math.log(YARN_FACTOR) + 1.0
TURN_GRID = 2.0**15
ROUND_MAGIC = 1.5 * 2.0**23

FLOPS = 2 * BATCH * SEQ * D_MODEL * FEATURES


def turns_per_position(i):
    base = ROPE_THETA ** (-i / PAIRS)
    ramp = min(max((i - RAMP_LOW) / (RAMP_HIGH - RAMP_LOW), 0.0), 1.0)
    return (base * (1.0 - ramp) + (base / YARN_FACTOR) * ramp) / (2.0 * math.pi)


def build_positions(nc, pool):
    pos_int = pool.tile([P, TILES], I32)
    nc.gpsimd.iota(pos_int[:], pattern=[[1, TILES]], base=0, channel_multiplier=TILES)
    pos = pool.tile([P, TILES], F32)
    nc.vector.tensor_copy(out=pos[:], in_=pos_int[:])
    return pos


def build_rope_squares(nc, pool, pos):
    sin_first = pool.tile([P, 1], F32)
    nc.scalar.activation(out=sin_first[:], in_=pos[:, 0:1], func=ACT.Sin, scale=0.0)

    turns = [turns_per_position(i) for i in range(PAIRS)]
    coarse_turns = [round(t * TURN_GRID) / TURN_GRID for t in turns]
    fast = sum(t != 0.0 for t in coarse_turns)
    coarse = pool.tile([P, fast, TILES], F32)
    fine = pool.tile([P, fast, TILES], F32)
    frac = pool.tile([P, 3, PAIRS, TILES], F32)
    for i in range(PAIRS):
        if i < fast:
            nc.vector.tensor_scalar(
                out=coarse[:, i, :], in0=pos[:], scalar1=coarse_turns[i], scalar2=None, op0=ALU.mult
            )
            nc.vector.tensor_scalar(
                out=fine[:, i, :], in0=pos[:], scalar1=turns[i] - coarse_turns[i], scalar2=None, op0=ALU.mult
            )
        else:
            nc.scalar.mul(out=frac[:, 0, i, :], in_=pos[:], mul=turns[i])

    whole = pool.tile([P, fast, TILES], F32)
    nc.vector.tensor_scalar(
        out=whole[:],
        in0=coarse[:],
        scalar1=ROUND_MAGIC,
        scalar2=ROUND_MAGIC,
        op0=ALU.add,
        op1=ALU.subtract,
    )
    nc.vector.tensor_tensor(out=coarse[:], in0=coarse[:], in1=whole[:], op=ALU.subtract)
    nc.vector.tensor_tensor(out=frac[:, 0, :fast], in0=coarse[:], in1=fine[:], op=ALU.add)
    nc.vector.tensor_scalar(out=frac[:, 1], in0=frac[:, 0], scalar1=-0.25, scalar2=None, op0=ALU.add)
    nc.vector.tensor_scalar(out=frac[:, 2], in0=frac[:, 0], scalar1=0.25, scalar2=None, op0=ALU.add)

    half_sine = pool.tile([P, 3, PAIRS, TILES], F32)
    nc.scalar.activation(out=half_sine[:], in_=frac[:], func=ACT.Sin, scale=math.pi)
    square = pool.tile([P, 3, PAIRS, TILES], F32)
    nc.vector.tensor_tensor(out=square[:], in0=half_sine[:], in1=half_sine[:], op=ALU.mult)
    return square


def finish_rope_tables(nc, square, table):
    nc.vector.tensor_scalar(
        out=table[:, :, 0].rearrange("p n j (i e) -> p n j i e", e=2),
        in0=square[:, 0]
        .rearrange("p i (n j) -> p n j i", j=CHUNK_TILES)
        .unsqueeze(4)
        .to_broadcast([P, CHUNKS, CHUNK_TILES, PAIRS, 2]),
        scalar1=-2.0 * ATTN_FACTOR,
        scalar2=ATTN_FACTOR,
        op0=ALU.mult,
        op1=ALU.add,
    )
    nc.vector.tensor_scalar(
        out=table[:, :, 1].rearrange("p n j (i e) -> p n j i e", e=2),
        in0=square[:, 1:3].rearrange("p e i (n j) -> p n j i e", j=CHUNK_TILES),
        scalar1=-2.0 * ATTN_FACTOR,
        scalar2=ATTN_FACTOR,
        op0=ALU.mult,
        op1=ALU.add,
    )


def tile_causalselfattentiongqa_pa_t_kernel(tc, x, w_qkv, out_0, out_1, out_2):
    nc = tc.nc
    with ExitStack() as ctx:
        const = ctx.enter_context(tc.tile_pool(name="const", bufs=1))
        x_pool = ctx.enter_context(tc.tile_pool(name="x", bufs=ALL_CHUNKS))
        reorder_pool = ctx.enter_context(tc.tile_pool(name="reorder", bufs=3))
        mx_pool = ctx.enter_context(tc.tile_pool(name="mx", bufs=3))
        rope_pool = ctx.enter_context(tc.tile_pool(name="rope", bufs=3))
        out_pool = ctx.enter_context(tc.tile_pool(name="out", bufs=STORES))
        psum_t = ctx.enter_context(tc.psum_pool(name="psum_t", bufs=6))
        psum_u = ctx.enter_context(tc.psum_pool(name="psum_u", bufs=2))
        ctx.enter_context(tc.manual_schedule())

        x_rows = x.rearrange("b (p j) d -> b p (j d)", j=TILES)
        x_chunks = {}
        reordered_tiles = {}
        mx_tiles = {}
        u_banks = {}
        rope_tiles = {}
        out_tiles = {}

        def load(n, parts, begin, end):
            b, c = divmod(n, CHUNKS)
            if begin == 0:
                x_chunk = x_pool.tile([P, CHUNK_TILES * D_MODEL], BF16)
                x_chunks[n] = x_chunk
            x_chunk = x_chunks[n]
            width = CHUNK_TILES * D_MODEL // parts
            for part in range(begin, end):
                lo = part * width
                first = c * CHUNK_TILES * D_MODEL + lo
                nc.sync.dma_start(out=x_chunk[:, lo : lo + width], in_=x_rows[b, :, first : first + width])

        def reorder(n):
            if FIRST_REORDERED <= n < ALL_CHUNKS:
                reordered = reorder_pool.tile([P, PASSES, WORD_BLOCKS, P], F32)
                first = REORDERED_TILE * TILE_WORDS
                words = x_chunks[n][:].bitcast(F32)[:, first : first + TILE_WORDS]
                nc.vector.tensor_copy(
                    out=reordered[:], in_=words.rearrange("p (g w u) -> p g u w", g=PASSES, u=WORD_BLOCKS)
                )
                reordered_tiles[n] = reordered

        def transpose(unit):
            n, lo, hi = unit
            if lo == 0:
                grouped = mx_pool.tile([P, CHUNK_TILES * PASSES * P * PACK], BF16, align_bytes=64)
                codes = mx_pool.tile([P, CHUNK_TILES * PASSES * P], U32, align_bytes=64)
                scales = mx_pool.tile([P, CHUNK_TILES * PASSES * P], U8, align_bytes=64)
                mx_tiles[n] = (grouped, codes, scales)
            grouped, codes, scales = mx_tiles[n]
            x_words = x_chunks[n][:].bitcast(F32)
            grouped_words = grouped[:].bitcast(F32).rearrange(
                "p (j g c u) -> p j g c u", j=CHUNK_TILES, g=PASSES, u=WORD_BLOCKS
            )
            for jj in range(lo, hi):
                xt = psum_t.tile([P, PASSES, WORD_BLOCKS, P], F32)
                for g in range(PASSES):
                    for u in range(WORD_BLOCKS):
                        if jj == REORDERED_TILE and n >= FIRST_REORDERED:
                            words = reordered_tiles[n][:, g, u, :]
                        else:
                            first = (jj * PASSES + g) * PASS_WORDS
                            words = x_words[:, first + u : first + PASS_WORDS : WORD_BLOCKS]
                        nc.tensor.transpose(xt[:, g, u, :], words, identity[:])
                nc.scalar.copy(out=grouped_words[:, jj], in_=xt[:].rearrange("p g u c -> p g c u"))

        def quantise(unit):
            n, lo, hi = unit
            grouped, codes, scales = mx_tiles[n]
            words = slice(lo * PASSES * P, hi * PASSES * P)
            nc.vector.quantize_mx(
                out=codes[:, words].bitcast(FP8X4),
                scales=scales[:, words],
                in_=grouped[:, lo * PASSES * P * PACK : hi * PASSES * P * PACK],
            )

        def project(unit):
            n, lo, hi = unit
            grouped, codes, scales = mx_tiles[n]
            u_bank = psum_u.tile([P, CHUNK_TILES, FEATURES], F32)
            for jj in range(lo, hi):
                for g in range(PASSES):
                    first = (jj * PASSES + g) * P
                    nc.tensor.matmul_mx(
                        out=u_bank[:, jj, :],
                        lhsT=codes[:, first : first + P].bitcast(FP8X4),
                        lhsT_scale=scales[:, first : first + P],
                        rhs=w_codes[:, g * FEATURES : (g + 1) * FEATURES].bitcast(FP8X4),
                        rhs_scale=w_scales[:, g * FEATURES : (g + 1) * FEATURES],
                        start=(g == 0),
                        stop=(g == PASSES - 1),
                    )
            u_banks[unit] = u_bank

        def rope_products(unit):
            n, lo, hi = unit
            tiles = hi - lo
            c = n % CHUNKS
            if c % STORE_CHUNKS == 0 and lo == 0:
                out_sb = out_pool.tile([P, HEADS, STORE_TILES, HEAD_DIM], F32)
                out_tiles[n // STORE_CHUNKS] = out_sb
            out_sb = out_tiles[n // STORE_CHUNKS]
            u_bank = u_banks[unit]
            j_store = (c % STORE_CHUNKS) * CHUNK_TILES + lo
            nc.scalar.copy(
                out=out_sb[:, ROPE_HEADS, j_store : j_store + tiles, :],
                in_=u_bank[:, lo:hi, ROPE_COLS:],
            )
            products = rope_pool.tile([P, 2, tiles, ROPE_COLS], F32)
            roped = u_bank[:, lo:hi, :ROPE_COLS].rearrange("p j (h d) -> p j h d", h=ROPE_HEADS)
            if tiles == CHUNK_TILES:
                both = [P, 2, tiles, ROPE_HEADS, HEAD_DIM]
                nc.vector.tensor_tensor(
                    out=products[:].rearrange("p s j (h d) -> p s j h d", h=ROPE_HEADS),
                    in0=roped.unsqueeze(1).to_broadcast(both),
                    in1=table[:, c].unsqueeze(3).to_broadcast(both),
                    op=ALU.mult,
                )
            else:
                for s in range(2):
                    nc.vector.tensor_tensor(
                        out=products[:, s].rearrange("p j (h d) -> p j h d", h=ROPE_HEADS),
                        in0=roped,
                        in1=table[:, c, s, lo:hi].unsqueeze(2).to_broadcast([P, tiles, ROPE_HEADS, HEAD_DIM]),
                        op=ALU.mult,
                    )
            rope_tiles[unit] = products

        def hold_sum(n, transposed):
            grouped, codes, scales = mx_tiles[transposed]
            j_store = (n % STORE_CHUNKS) * CHUNK_TILES
            width = CHUNK_TILES * PASSES * P * PACK
            nc.vector.tensor_copy(
                out=out_tiles[n // STORE_CHUNKS][:, 0, j_store, 0:1], in_=grouped[:, width - 1 : width]
            )

        def rope_sum(unit, engine=nc.vector):
            n, lo, hi = unit
            out_sb = out_tiles[n // STORE_CHUNKS]
            products = rope_tiles[unit]
            j_store = (n % STORE_CHUNKS) * CHUNK_TILES + lo
            pairs = products[:].rearrange("p s j (h i e) -> p s j h i e", h=ROPE_HEADS, e=2)
            engine.tensor_tensor(
                out=out_sb[:, :ROPE_HEADS, j_store : j_store + hi - lo, :].rearrange(
                    "p h j (i e) -> p j h i e", e=2
                ),
                in0=pairs[:, 0],
                in1=pairs[:, 1, :, :, :, ::-1],
                op=ALU.add,
            )

        def store(n, lo, hi):
            b, c = divmod(n, CHUNKS)
            out_sb = out_tiles[n // STORE_CHUNKS]
            in_batch = slice(c * CHUNK_TILES + lo, c * CHUNK_TILES + hi)
            nc.sync.dma_start(
                out=out_2[b, 0].rearrange("(p j) d -> p j d", j=TILES)[:, in_batch, :],
                in_=out_sb[:, 3, lo:hi],
            )
            nc.sync.dma_start(
                out=out_0[b, 0].rearrange("h (p j) d -> p h j d", j=TILES)[:, :, in_batch, :],
                in_=out_sb[:, 0:2, lo:hi],
            )
            nc.sync.dma_start(
                out=out_1[b, 0].rearrange("(p j) d -> p j d", j=TILES)[:, in_batch, :],
                in_=out_sb[:, 2, lo:hi],
            )

        load(0, CHUNK_TILES, 0, CHUNK_TILES)
        load(1, CHUNK_TILES, 0, HALF_TILES)
        w_raw = const.tile([P, PASSES, PACK, FEATURES], BF16)
        nc.sync.dma_start(
            out=w_raw[:].rearrange("p g t c -> p g (t c)"),
            in_=w_qkv.rearrange("(g p t) c -> p g (t c)", p=P, t=PACK),
        )
        load(1, CHUNK_TILES, HALF_TILES, CHUNK_TILES)
        for n in range(2, ALL_CHUNKS):
            parts = HALVES if n < EARLY_CHUNKS else 1
            load(n, parts, 0, parts)

        pos = build_positions(nc, const)
        square = build_rope_squares(nc, const, pos)
        table = const.tile([P, CHUNKS, 2, CHUNK_TILES, HEAD_DIM], F32)
        finish_rope_tables(nc, square, table)

        identity = const.tile([P, P], F32)
        make_identity(nc, identity[:])

        w_grouped = const.tile([P, PASSES, FEATURES, PACK], BF16, align_bytes=64)
        w_codes = const.tile([P, PASSES * FEATURES], U32, align_bytes=64)
        w_scales = const.tile([P, PASSES * FEATURES], U8, align_bytes=64)

        def quantise_weights():
            nc.vector.tensor_copy(out=w_grouped[:], in_=w_raw[:].rearrange("p g t c -> p g c t"))
            nc.vector.quantize_mx(
                out=w_codes[:].bitcast(FP8X4),
                scales=w_scales[:],
                in_=w_grouped[:].rearrange("p g c t -> p (g c t)"),
            )

        def whole(n):
            return (n, 0, CHUNK_TILES)

        def first_half(n):
            return (n, 0, HALF_TILES)

        def second_half(n):
            return (n, HALF_TILES, CHUNK_TILES)

        last = ALL_CHUNKS - 1
        for n in range(last):
            transpose(first_half(n))
            quantise(first_half(n))
            transpose(second_half(n))
            if 0 <= n - 2:
                hold_sum(n - 2, n)
            quantise(second_half(n))
            if n == 0:
                quantise_weights()
            if 0 <= n - 1:
                project(whole(n - 1))
                rope_products(whole(n - 1))
            if 0 <= n - 2:
                rope_sum(whole(n - 2), nc.gpsimd)
                if (n - 2) % STORE_CHUNKS == STORE_CHUNKS - 1:
                    store(n - 1 - STORE_CHUNKS, 0, STORE_TILES)
            reorder(n + 2)

        transpose(first_half(last))
        quantise(first_half(last))
        transpose(second_half(last))
        project(whole(last - 1))
        hold_sum(last - 2, last)
        quantise(second_half(last))
        rope_products(whole(last - 1))
        rope_sum(whole(last - 2), nc.gpsimd)
        store(last - 3, 0, STORE_TILES)
        project(first_half(last))
        rope_products(first_half(last))
        rope_sum(whole(last - 1), nc.gpsimd)
        store(last - 1, 0, CHUNK_TILES)
        project(second_half(last))
        rope_products(second_half(last))
        rope_sum(first_half(last))
        rope_sum(second_half(last))
        store(last - 1, CHUNK_TILES, STORE_TILES)
